import numpy as np
import ml_dtypes


def mxq(x, axis, fmt="e4m3"):
    dtype, down = {"e4m3": (ml_dtypes.float8_e4m3fn, 7), "e5m2": (ml_dtypes.float8_e5m2, 14)}[fmt]
    v = np.moveaxis(np.asarray(x, np.float32).astype(ml_dtypes.bfloat16).astype(np.float64), axis, -1)
    blocks = v.reshape(v.shape[:-1] + (-1, 32))
    amax = np.abs(blocks).max(-1, keepdims=True)
    byte = np.maximum(np.where(amax > 0, np.frexp(amax)[1] - 1 + 127, 0) - down, 1)
    scale = np.exp2(byte - 127.0)
    codes = (blocks / scale).astype(np.float32).astype(dtype).astype(np.float64)
    return np.moveaxis((codes * scale).reshape(v.shape), -1, axis)


WIDE = False


def mx_kscale(k):
    if not WIDE:
        return np.ones(k)
    levels = np.array([10, -10, 5, -5, 0])
    a = np.random.permutation(np.resize(levels, k // 512 * 4)).reshape(k // 512, 4)
    idx = np.arange(k)
    return np.exp2(a[idx // 512, idx % 128 // 32])


BF16 = ml_dtypes.bfloat16


def bf(x):
    return np.asarray(x, np.float32).astype(BF16)


def f64(x):
    return np.asarray(x).astype(np.float64)


B, S, D, H, DH, DR, DKV, DQ = 2, 4096, 512, 2, 128, 64, 512, 512
HALF = DR // 2


def rope(t, cos, sin):
    t1, t2 = t[..., 0::2], t[..., 1::2]
    c = cos[None, :, None, :]
    s = sin[None, :, None, :]
    return np.stack([t1 * c - t2 * s, t1 * s + t2 * c], axis=-1).reshape(t.shape)


def setup_inputs():
    s, t = mx_kscale(D), mx_kscale(DQ)
    ang = np.random.uniform(0.0, 2.0 * np.pi, (S, HALF))
    return {"x": bf(np.random.standard_normal((B, S, D)) * s),
            "W_q_down": bf(np.random.standard_normal((D, DQ)) / np.sqrt(D) / s[:, None] * t),
            "W_q_up": bf(np.random.standard_normal((DQ, H * DH)) / np.sqrt(DQ) / t[:, None]),
            "W_q_rope": bf(np.random.standard_normal((DQ, H * DR)) / np.sqrt(DQ) / t[:, None]),
            "rope_cos": bf(np.cos(ang)), "rope_sin": bf(np.sin(ang))}


def reference(x, W_q_down, W_q_up, W_q_rope, rope_cos, rope_sin):
    down_q = mxq(f64(x), 2, "e4m3") @ mxq(f64(W_q_down), 0, "e4m3")
    dq = mxq(down_q, 2, "e4m3")
    q_c = (dq @ mxq(f64(W_q_up), 0, "e4m3")).reshape(B, S, H, DH)
    q_r = (dq @ mxq(f64(W_q_rope), 0, "e4m3")).reshape(B, S, H, DR)
    q_r = rope(q_r, f64(rope_cos), f64(rope_sin))
    return np.concatenate([q_c, q_r], axis=-1).transpose(0, 2, 1, 3)

@@ -1,0 +1,283 @@
+from contextlib import ExitStack
+
+import concourse.mybir as mybir
+from concourse.masks import make_identity
+
+F32 = mybir.dt.float32
+BF16 = mybir.dt.bfloat16
+U32 = mybir.dt.uint32
+U8 = mybir.dt.uint8
+FP8X4 = mybir.dt.float8_e4m3fn_x4
+MULT = mybir.AluOpType.mult
+ADD = mybir.AluOpType.add
+
+P = 128
+PACK = 4
+BANK = 512
+
+BATCH, SEQ, D = 2, 4096, 512
+DQ = 512
+HEADS, DH, DR = 2, 128, 64
+PAIRS = DR // 2
+N_UP = HEADS * DH
+N_ROPE = HEADS * DR
+D_OUT = DH + DR
+
+TILES = 4
+GROUP = TILES * P
+N_GROUPS = BATCH * SEQ // GROUP
+SEQ_GROUPS = SEQ // GROUP
+WORDS = D // 2
+
+FLOPS = 2 * BATCH * SEQ * (D * DQ + DQ * (N_UP + N_ROPE))
+
+
+def tile_multiheadlatentattention_pa_t_kernel(
+    tc, x, W_q_down, W_q_up, W_q_rope, rope_cos, rope_sin, out
+):
+    nc = tc.nc
+    x_rows = x.flatten_outer_dims()
+
+    with ExitStack() as ctx:
+        consts = ctx.enter_context(tc.tile_pool(name="consts", bufs=1))
+        x_pool = ctx.enter_context(tc.tile_pool(name="x_pool", bufs=N_GROUPS))
+        stage = ctx.enter_context(tc.tile_pool(name="stage", bufs=2))
+        packed = ctx.enter_context(tc.tile_pool(name="packed", bufs=4))
+        results = ctx.enter_context(tc.tile_pool(name="results", bufs=5))
+        psum = ctx.enter_context(tc.psum_pool(name="psum", bufs=8))
+        ctx.enter_context(tc.manual_schedule())
+
+        x_tiles = []
+
+        def load_x(g):
+            x_sb = x_pool.tile([P, TILES * D], BF16)
+            rows = x_rows[g * GROUP : (g + 1) * GROUP, :]
+            nc.sync.dma_start(out=x_sb[:], in_=rows.rearrange("(p j) k -> p (j k)", j=TILES))
+            x_tiles.append(x_sb)
+
+        raw_down = consts.tile([P, PACK, DQ], BF16)
+        nc.sync.dma_start(
+            out=raw_down[:].rearrange("p (u e) f -> p u (e f)", u=2),
+            in_=W_q_down.rearrange("(u p e) f -> p u (e f)", u=2, e=2),
+        )
+        load_x(0)
+        raw_up = consts.tile([P, PACK, N_UP], BF16)
+        nc.sync.dma_start(out=raw_up[:], in_=W_q_up.rearrange("(p t) n -> p t n", t=PACK))
+        raw_rope = consts.tile([P, PACK, N_ROPE], BF16)
+        nc.sync.dma_start(out=raw_rope[:], in_=W_q_rope.rearrange("(p t) n -> p t n", t=PACK))
+        load_x(1)
+        cos_sb = consts.tile([P, SEQ_GROUPS, TILES, PAIRS], BF16)
+        nc.sync.dma_start(
+            out=cos_sb[:].rearrange("p g j i -> p g (j i)"),
+            in_=rope_cos.rearrange("(g p j) i -> p g (j i)", p=P, j=TILES),
+        )
+        sin_sb = consts.tile([P, SEQ_GROUPS, TILES, PAIRS], BF16)
+        nc.sync.dma_start(
+            out=sin_sb[:].rearrange("p g j i -> p g (j i)"),
+            in_=rope_sin.rearrange("(g p j) i -> p g (j i)", p=P, j=TILES),
+        )
+        for g in range(2, N_GROUPS):
+            load_x(g)
+
+        identity = consts.tile([P, P], F32)
+        make_identity(nc, identity[:])
+
+        grouped_down = consts.tile([P, PACK, P, PACK], BF16, align_bytes=64)
+        down_view = raw_down[:].rearrange("p k (q t) -> p t q k", t=PACK)
+        nc.vector.tensor_copy(out=grouped_down[:, 0:2], in_=down_view[:, 0:2])
+        nc.scalar.copy(out=grouped_down[:, 2:4], in_=down_view[:, 2:4])
+        down_codes = consts.tile([P, DQ], U32, align_bytes=64)
+        down_scales = consts.tile([P, DQ], U8, align_bytes=64)
+        nc.vector.quantize_mx(
+            out=down_codes[:].bitcast(FP8X4),
+            scales=down_scales[:],
+            in_=grouped_down[:].rearrange("p t q k -> p (t q k)"),
+        )
+
+        grouped_up = consts.tile([P, N_UP, PACK], BF16, align_bytes=64)
+        nc.scalar.copy(out=grouped_up[:], in_=raw_up[:].rearrange("p k n -> p n k"))
+        grouped_rope = consts.tile([P, N_ROPE, PACK], BF16, align_bytes=64)
+        nc.scalar.copy(
+            out=grouped_rope[:].rearrange("p (e n) k -> p e n k", e=2),
+            in_=raw_rope[:].rearrange("p k (n e) -> p e n k", e=2),
+        )
+        second_codes = consts.tile([P, N_UP + N_ROPE], U32, align_bytes=64)
+        second_scales = consts.tile([P, N_UP + N_ROPE], U8, align_bytes=64)
+        minus_sin = consts.tile([P, SEQ_GROUPS, TILES, PAIRS], BF16)
+
+        def prepare_second_weights():
+            nc.vector.quantize_mx(
+                out=second_codes[:, 0:N_UP].bitcast(FP8X4),
+                scales=second_scales[:, 0:N_UP],
+                in_=grouped_up[:].rearrange("p n k -> p (n k)"),
+            )
+            nc.vector.quantize_mx(
+                out=second_codes[:, N_UP:].bitcast(FP8X4),
+                scales=second_scales[:, N_UP:],
+                in_=grouped_rope[:].rearrange("p n k -> p (n k)"),
+            )
+            nc.vector.tensor_scalar_mul(out=minus_sin[:], in0=sin_sb[:], scalar1=-1.0)
+
+        x_banks, x_grouped, x_packed = {}, {}, {}
+        latent_grouped, latent_packed = {}, {}
+        plain_banks, rope_banks, products, result_tiles = {}, {}, {}, {}
+
+        def transpose_x(g):
+            words = x_tiles[g][:].bitcast(F32)
+            x_banks[g] = []
+            for half in range(2):
+                xt = psum.tile([P, 2, 2, P], F32, tag="bank")
+                for jj in range(2):
+                    for u in range(2):
+                        first = (2 * half + jj) * WORDS + u * P
+                        nc.tensor.transpose(xt[:, jj, u, :], words[:, first : first + P], identity[:])
+                x_banks[g].append(xt)
+
+        def copy_x(g):
+            gx = stage.tile([P, GROUP * PACK], BF16, align_bytes=64)
+            gx_words = gx[:].bitcast(F32).rearrange("p (j r u) -> p j r u", j=TILES, u=2)
+            for half in range(2):
+                nc.vector.tensor_copy(
+                    out=gx_words[:, 2 * half : 2 * half + 2],
+                    in_=x_banks[g][half][:].rearrange("p j u r -> p j r u"),
+                )
+            x_grouped[g] = gx
+
+        def quantise(grouped):
+            codes = packed.tile([P, GROUP], U32, align_bytes=64)
+            scales = packed.tile([P, GROUP], U8, align_bytes=64)
+            nc.vector.quantize_mx(out=codes[:].bitcast(FP8X4), scales=scales[:], in_=grouped[:])
+            return codes, scales
+
+        def first_product(g):
+            codes, scales = x_packed[g]
+            gq = stage.tile([P, GROUP * PACK], BF16, align_bytes=64)
+            for j in range(TILES):
+                tokens = slice(j * P, (j + 1) * P)
+                latent = psum.tile([P, PACK, P], F32, tag="bank")
+                for t in range(PACK):
+                    features = slice(t * P, (t + 1) * P)
+                    nc.tensor.matmul_mx(
+                        out=latent[:, t, :],
+                        lhsT=down_codes[:, features].bitcast(FP8X4),
+                        lhsT_scale=down_scales[:, features],
+                        rhs=codes[:, tokens].bitcast(FP8X4),
+                        rhs_scale=scales[:, tokens],
+                        start=True,
+                        stop=True,
+                    )
+                nc.scalar.copy(
+                    out=gq[:, j * BANK : (j + 1) * BANK].rearrange("p (r t) -> p r t", t=PACK),
+                    in_=latent[:].rearrange("p t r -> p r t"),
+                )
+            latent_grouped[g] = gq
+
+        def second_products(g):
+            codes, scales = latent_packed[g]
+            plain_banks[g] = []
+            rope_bank = psum.tile([P, TILES, N_ROPE], F32, tag="bank")
+            for j in range(TILES):
+                tokens = slice(j * P, (j + 1) * P)
+                if j % 2 == 0:
+                    plain_bank = psum.tile([P, 2, N_UP], F32, tag="bank")
+                    plain_banks[g].append(plain_bank)
+                nc.tensor.matmul_mx(
+                    out=plain_bank[:, j % 2, :],
+                    lhsT=codes[:, tokens].bitcast(FP8X4),
+                    lhsT_scale=scales[:, tokens],
+                    rhs=second_codes[:, 0:N_UP].bitcast(FP8X4),
+                    rhs_scale=second_scales[:, 0:N_UP],
+                    start=True,
+                    stop=True,
+                )
+                nc.tensor.matmul_mx(
+                    out=rope_bank[:, j, :],
+                    lhsT=codes[:, tokens].bitcast(FP8X4),
+                    lhsT_scale=scales[:, tokens],
+                    rhs=second_codes[:, N_UP:].bitcast(FP8X4),
+                    rhs_scale=second_scales[:, N_UP:],
+                    start=True,
+                    stop=True,
+                )
+            rope_banks[g] = rope_bank
+
+        def copy_plain(g):
+            res = results.tile([P, HEADS, TILES, D_OUT], F32)
+            for half in range(2):
+                nc.scalar.copy(
+                    out=res[:, :, 2 * half : 2 * half + 2, 0:DH].rearrange("p h j c -> p j h c"),
+                    in_=plain_banks[g][half][:].rearrange("p j (h c) -> p j h c", h=HEADS),
+                )
+            result_tiles[g] = res
+
+        def rotary_products(g):
+            tables = g % SEQ_GROUPS
+            q_r = rope_banks[g][:].rearrange("p j (a i) -> p j a i", i=PAIRS)
+            by_cos = stage.tile([P, 2 * HEADS, TILES, PAIRS], F32)
+            by_sin = stage.tile([P, 2 * HEADS, TILES, PAIRS], F32)
+            cos_g = cos_sb[:, tables].unsqueeze(2)
+            sin_g = sin_sb[:, tables].unsqueeze(2)
+            minus_sin_g = minus_sin[:, tables].unsqueeze(2)
+            nc.vector.tensor_tensor(
+                out=by_cos[:].rearrange("p a j i -> p j a i"),
+                in0=q_r,
+                in1=cos_g.to_broadcast([P, TILES, 2 * HEADS, PAIRS]),
+                op=MULT,
+            )
+            nc.vector.tensor_tensor(
+                out=by_sin[:, 0:HEADS].rearrange("p h j i -> p j h i"),
+                in0=q_r[:, :, HEADS:, :],
+                in1=minus_sin_g.to_broadcast([P, TILES, HEADS, PAIRS]),
+                op=MULT,
+            )
+            nc.vector.tensor_tensor(
+                out=by_sin[:, HEADS:].rearrange("p h j i -> p j h i"),
+                in0=q_r[:, :, 0:HEADS, :],
+                in1=sin_g.to_broadcast([P, TILES, HEADS, PAIRS]),
+                op=MULT,
+            )
+            products[g] = (by_cos, by_sin)
+
+        def rotary_sum_and_store(g):
+            by_cos, by_sin = products[g]
+            res = result_tiles[g]
+            nc.vector.tensor_tensor(
+                out=res[:, :, :, DH:].rearrange("p h j (i e) -> p (h j) i e", e=2),
+                in0=by_cos[:].rearrange("p (e h) j i -> p (h j) i e", e=2),
+                in1=by_sin[:].rearrange("p (e h) j i -> p (h j) i e", e=2),
+                op=ADD,
+            )
+            first = (g % SEQ_GROUPS) * GROUP
+            rows = out[g // SEQ_GROUPS, :, first : first + GROUP, :]
+            nc.sync.dma_start(
+                out=rows.rearrange("h (p j) c -> p h (j c)", j=TILES),
+                in_=res[:].rearrange("p h j c -> p h (j c)"),
+            )
+
+        def live(g):
+            return 0 <= g < N_GROUPS
+
+        def step(i):
+            if live(i):
+                latent_packed[i] = quantise(latent_grouped[i])
+            if live(i + 2):
+                transpose_x(i + 2)
+            if live(i - 1):
+                rotary_products(i - 1)
+                copy_plain(i - 1)
+            if live(i + 1):
+                first_product(i + 1)
+            if live(i + 2):
+                copy_x(i + 2)
+            if live(i - 1):
+                rotary_sum_and_store(i - 1)
+            if live(i):
+                second_products(i)
+            if live(i + 2):
+                x_packed[i + 2] = quantise(x_grouped[i + 2])
+
+        step(-2)
+        step(-1)
+        prepare_second_weights()
+        for i in range(N_GROUPS + 1):
+            step(i)

@@ -146,7 +146,13 @@ def tile_multiheadlatentattention_pa_t_kernel(
         def quantise(grouped):
             codes = packed.tile([P, GROUP], U32, align_bytes=64)
             scales = packed.tile([P, GROUP], U8, align_bytes=64)
-            nc.vector.quantize_mx(out=codes[:].bitcast(FP8X4), scales=scales[:], in_=grouped[:])
+            for half in range(2):
+                cols = slice(half * GROUP // 2, (half + 1) * GROUP // 2)
+                nc.vector.quantize_mx(
+                    out=codes[:, cols].bitcast(FP8X4),
+                    scales=scales[:, cols],
+                    in_=grouped[:, half * GROUP * PACK // 2 : (half + 1) * GROUP * PACK // 2],
+                )
             return codes, scales
 
         def first_product(g):
@@ -241,18 +247,19 @@ def tile_multiheadlatentattention_pa_t_kernel(
         def rotary_sum_and_store(g):
             by_cos, by_sin = products[g]
             res = result_tiles[g]
-            nc.vector.tensor_tensor(
-                out=res[:, :, :, DH:].rearrange("p h j (i e) -> p (h j) i e", e=2),
-                in0=by_cos[:].rearrange("p (e h) j i -> p (h j) i e", e=2),
-                in1=by_sin[:].rearrange("p (e h) j i -> p (h j) i e", e=2),
-                op=ADD,
-            )
             first = (g % SEQ_GROUPS) * GROUP
-            rows = out[g // SEQ_GROUPS, :, first : first + GROUP, :]
-            nc.sync.dma_start(
-                out=rows.rearrange("h (p j) c -> p h (j c)", j=TILES),
-                in_=res[:].rearrange("p h j c -> p h (j c)"),
-            )
+            for h in range(HEADS):
+                nc.gpsimd.tensor_tensor(
+                    out=res[:, h, :, DH:].rearrange("p j (i e) -> p j i e", e=2),
+                    in0=by_cos[:].rearrange("p (e h) j i -> p h j i e", e=2)[:, h],
+                    in1=by_sin[:].rearrange("p (e h) j i -> p h j i e", e=2)[:, h],
+                    op=ADD,
+                )
+                rows = out[g // SEQ_GROUPS, h, first : first + GROUP, :]
+                nc.sync.dma_start(
+                    out=rows.rearrange("(p j) c -> p (j c)", j=TILES),
+                    in_=res[:, h].rearrange("p j c -> p (j c)"),
+                )
 
         def live(g):
             return 0 <= g < N_GROUPS
@@ -265,12 +272,11 @@ def tile_multiheadlatentattention_pa_t_kernel(
             if live(i - 1):
                 rotary_products(i - 1)
                 copy_plain(i - 1)
+                rotary_sum_and_store(i - 1)
             if live(i + 1):
                 first_product(i + 1)
             if live(i + 2):
                 copy_x(i + 2)
-            if live(i - 1):
-                rotary_sum_and_store(i - 1)
             if live(i):
                 second_products(i)
             if live(i + 2):

@@ -14,6 +14,7 @@ ADD = mybir.AluOpType.add
 P = 128
 PACK = 4
 BANK = 512
+PSUM_BANKS = 8
 
 BATCH, SEQ, D = 2, 4096, 512
 DQ = 512
@@ -22,12 +23,14 @@ PAIRS = DR // 2
 N_UP = HEADS * DH
 N_ROPE = HEADS * DR
 D_OUT = DH + DR
+WORDS = D // 2
 
-TILES = 4
+TILES = BANK // N_ROPE
 GROUP = TILES * P
 N_GROUPS = BATCH * SEQ // GROUP
 SEQ_GROUPS = SEQ // GROUP
-WORDS = D // 2
+HALVES = 2
+HALF_TILES = TILES // HALVES
 
 FLOPS = 2 * BATCH * SEQ * (D * DQ + DQ * (N_UP + N_ROPE))
 
@@ -41,10 +44,10 @@ def tile_multiheadlatentattention_pa_t_kernel(
     with ExitStack() as ctx:
         consts = ctx.enter_context(tc.tile_pool(name="consts", bufs=1))
         x_pool = ctx.enter_context(tc.tile_pool(name="x_pool", bufs=N_GROUPS))
-        stage = ctx.enter_context(tc.tile_pool(name="stage", bufs=2))
-        packed = ctx.enter_context(tc.tile_pool(name="packed", bufs=4))
+        stage = ctx.enter_context(tc.tile_pool(name="stage", bufs=3))
+        packed = ctx.enter_context(tc.tile_pool(name="packed", bufs=6))
         results = ctx.enter_context(tc.tile_pool(name="results", bufs=5))
-        psum = ctx.enter_context(tc.psum_pool(name="psum", bufs=8))
+        psum = ctx.enter_context(tc.psum_pool(name="psum", bufs=PSUM_BANKS))
         ctx.enter_context(tc.manual_schedule())
 
         x_tiles = []
@@ -57,14 +60,14 @@ def tile_multiheadlatentattention_pa_t_kernel(
 
         raw_down = consts.tile([P, PACK, DQ], BF16)
         nc.sync.dma_start(
-            out=raw_down[:].rearrange("p (u e) f -> p u (e f)", u=2),
-            in_=W_q_down.rearrange("(u p e) f -> p u (e f)", u=2, e=2),
+            out=raw_down[:].rearrange("p (u m) f -> p u (m f)", u=2),
+            in_=W_q_down.rearrange("(u p m) f -> p u (m f)", u=2, m=2),
         )
         load_x(0)
         raw_up = consts.tile([P, PACK, N_UP], BF16)
-        nc.sync.dma_start(out=raw_up[:], in_=W_q_up.rearrange("(p t) n -> p t n", t=PACK))
+        nc.sync.dma_start(out=raw_up[:], in_=W_q_up.rearrange("(p k) n -> p k n", k=PACK))
         raw_rope = consts.tile([P, PACK, N_ROPE], BF16)
-        nc.sync.dma_start(out=raw_rope[:], in_=W_q_rope.rearrange("(p t) n -> p t n", t=PACK))
+        nc.sync.dma_start(out=raw_rope[:], in_=W_q_rope.rearrange("(p k) n -> p k n", k=PACK))
         load_x(1)
         cos_sb = consts.tile([P, SEQ_GROUPS, TILES, PAIRS], BF16)
         nc.sync.dma_start(
@@ -125,20 +128,20 @@ def tile_multiheadlatentattention_pa_t_kernel(
         def transpose_x(g):
             words = x_tiles[g][:].bitcast(F32)
             x_banks[g] = []
-            for half in range(2):
-                xt = psum.tile([P, 2, 2, P], F32, tag="bank")
-                for jj in range(2):
+            for half in range(HALVES):
+                xt = psum.tile([P, HALF_TILES, 2, P], F32, tag="bank")
+                for jj in range(HALF_TILES):
                     for u in range(2):
-                        first = (2 * half + jj) * WORDS + u * P
-                        nc.tensor.transpose(xt[:, jj, u, :], words[:, first : first + P], identity[:])
+                        word = (half * HALF_TILES + jj) * WORDS + u * P
+                        nc.tensor.transpose(xt[:, jj, u, :], words[:, word : word + P], identity[:])
                 x_banks[g].append(xt)
 
         def copy_x(g):
             gx = stage.tile([P, GROUP * PACK], BF16, align_bytes=64)
             gx_words = gx[:].bitcast(F32).rearrange("p (j r u) -> p j r u", j=TILES, u=2)
-            for half in range(2):
+            for half in range(HALVES):
                 nc.vector.tensor_copy(
-                    out=gx_words[:, 2 * half : 2 * half + 2],
+                    out=gx_words[:, half * HALF_TILES : (half + 1) * HALF_TILES],
                     in_=x_banks[g][half][:].rearrange("p j u r -> p j r u"),
                 )
             x_grouped[g] = gx
@@ -146,12 +149,14 @@ def tile_multiheadlatentattention_pa_t_kernel(
         def quantise(grouped):
             codes = packed.tile([P, GROUP], U32, align_bytes=64)
             scales = packed.tile([P, GROUP], U8, align_bytes=64)
-            for half in range(2):
-                cols = slice(half * GROUP // 2, (half + 1) * GROUP // 2)
+            half_group = GROUP // HALVES
+            for half in range(HALVES):
+                tokens = slice(half * half_group, (half + 1) * half_group)
+                values = slice(half * half_group * PACK, (half + 1) * half_group * PACK)
                 nc.vector.quantize_mx(
-                    out=codes[:, cols].bitcast(FP8X4),
-                    scales=scales[:, cols],
-                    in_=grouped[:, half * GROUP * PACK // 2 : (half + 1) * GROUP * PACK // 2],
+                    out=codes[:, tokens].bitcast(FP8X4),
+                    scales=scales[:, tokens],
+                    in_=grouped[:, values],
                 )
             return codes, scales
 
@@ -184,11 +189,11 @@ def tile_multiheadlatentattention_pa_t_kernel(
             rope_bank = psum.tile([P, TILES, N_ROPE], F32, tag="bank")
             for j in range(TILES):
                 tokens = slice(j * P, (j + 1) * P)
-                if j % 2 == 0:
-                    plain_bank = psum.tile([P, 2, N_UP], F32, tag="bank")
+                if j % HALF_TILES == 0:
+                    plain_bank = psum.tile([P, HALF_TILES, N_UP], F32, tag="bank")
                     plain_banks[g].append(plain_bank)
                 nc.tensor.matmul_mx(
-                    out=plain_bank[:, j % 2, :],
+                    out=plain_bank[:, j % HALF_TILES, :],
                     lhsT=codes[:, tokens].bitcast(FP8X4),
                     lhsT_scale=scales[:, tokens],
                     rhs=second_codes[:, 0:N_UP].bitcast(FP8X4),
@@ -209,9 +214,10 @@ def tile_multiheadlatentattention_pa_t_kernel(
 
         def copy_plain(g):
             res = results.tile([P, HEADS, TILES, D_OUT], F32)
-            for half in range(2):
+            for half in range(HALVES):
+                tiles = slice(half * HALF_TILES, (half + 1) * HALF_TILES)
                 nc.scalar.copy(
-                    out=res[:, :, 2 * half : 2 * half + 2, 0:DH].rearrange("p h j c -> p j h c"),
+                    out=res[:, :, tiles, 0:DH].rearrange("p h j c -> p j h c"),
                     in_=plain_banks[g][half][:].rearrange("p j (h c) -> p j h c", h=HEADS),
                 )
             result_tiles[g] = res
@@ -244,10 +250,10 @@ def tile_multiheadlatentattention_pa_t_kernel(
             )
             products[g] = (by_cos, by_sin)
 
-        def rotary_sum_and_store(g):
+        def rotary_sums_and_stores(g):
             by_cos, by_sin = products[g]
             res = result_tiles[g]
-            first = (g % SEQ_GROUPS) * GROUP
+            position = (g % SEQ_GROUPS) * GROUP
             for h in range(HEADS):
                 nc.gpsimd.tensor_tensor(
                     out=res[:, h, :, DH:].rearrange("p j (i e) -> p j i e", e=2),
@@ -255,7 +261,7 @@ def tile_multiheadlatentattention_pa_t_kernel(
                     in1=by_sin[:].rearrange("p (e h) j i -> p h j i e", e=2)[:, h],
                     op=ADD,
                 )
-                rows = out[g // SEQ_GROUPS, h, first : first + GROUP, :]
+                rows = out[g // SEQ_GROUPS, h, position : position + GROUP, :]
                 nc.sync.dma_start(
                     out=rows.rearrange("(p j) c -> p (j c)", j=TILES),
                     in_=res[:, h].rearrange("p j c -> p (j c)"),
@@ -264,26 +270,26 @@ def tile_multiheadlatentattention_pa_t_kernel(
         def live(g):
             return 0 <= g < N_GROUPS
 
-        def step(i):
-            if live(i):
-                latent_packed[i] = quantise(latent_grouped[i])
-            if live(i + 2):
-                transpose_x(i + 2)
-            if live(i - 1):
-                rotary_products(i - 1)
-                copy_plain(i - 1)
-                rotary_sum_and_store(i - 1)
-            if live(i + 1):
-                first_product(i + 1)
-            if live(i + 2):
-                copy_x(i + 2)
-            if live(i):
-                second_products(i)
-            if live(i + 2):
-                x_packed[i + 2] = quantise(x_grouped[i + 2])
+        def step(n):
+            if live(n + 2):
+                transpose_x(n + 2)
+            if live(n - 2):
+                rotary_products(n - 2)
+                copy_plain(n - 2)
+                rotary_sums_and_stores(n - 2)
+            if live(n + 1):
+                first_product(n + 1)
+            if live(n + 2):
+                copy_x(n + 2)
+            if live(n - 1):
+                second_products(n - 1)
+            if live(n + 2):
+                x_packed[n + 2] = quantise(x_grouped[n + 2])
+            if live(n):
+                latent_packed[n] = quantise(latent_grouped[n])
 
         step(-2)
         step(-1)
         prepare_second_weights()
-        for i in range(N_GROUPS + 1):
-            step(i)
+        for n in range(N_GROUPS + 2):
+            step(n)

@@ -45,6 +45,7 @@ def tile_multiheadlatentattention_pa_t_kernel(
         consts = ctx.enter_context(tc.tile_pool(name="consts", bufs=1))
         x_pool = ctx.enter_context(tc.tile_pool(name="x_pool", bufs=N_GROUPS))
         stage = ctx.enter_context(tc.tile_pool(name="stage", bufs=3))
+        planes = ctx.enter_context(tc.tile_pool(name="planes", bufs=2 * HEADS))
         packed = ctx.enter_context(tc.tile_pool(name="packed", bufs=6))
         results = ctx.enter_context(tc.tile_pool(name="results", bufs=5))
         psum = ctx.enter_context(tc.psum_pool(name="psum", bufs=PSUM_BANKS))
@@ -100,10 +101,11 @@ def tile_multiheadlatentattention_pa_t_kernel(
         grouped_up = consts.tile([P, N_UP, PACK], BF16, align_bytes=64)
         nc.scalar.copy(out=grouped_up[:], in_=raw_up[:].rearrange("p k n -> p n k"))
         grouped_rope = consts.tile([P, N_ROPE, PACK], BF16, align_bytes=64)
-        nc.scalar.copy(
-            out=grouped_rope[:].rearrange("p (e n) k -> p e n k", e=2),
-            in_=raw_rope[:].rearrange("p k (n e) -> p e n k", e=2),
-        )
+        for h in range(HEADS):
+            nc.scalar.copy(
+                out=grouped_rope[:, h * DR : (h + 1) * DR, :].rearrange("p (e i) k -> p e i k", e=2),
+                in_=raw_rope[:, :, h * DR : (h + 1) * DR].rearrange("p k (i e) -> p e i k", e=2),
+            )
         second_codes = consts.tile([P, N_UP + N_ROPE], U32, align_bytes=64)
         second_scales = consts.tile([P, N_UP + N_ROPE], U8, align_bytes=64)
         minus_sin = consts.tile([P, SEQ_GROUPS, TILES, PAIRS], BF16)
@@ -224,41 +226,35 @@ def tile_multiheadlatentattention_pa_t_kernel(
 
         def rotary_products(g):
             tables = g % SEQ_GROUPS
-            q_r = rope_banks[g][:].rearrange("p j (a i) -> p j a i", i=PAIRS)
-            by_cos = stage.tile([P, 2 * HEADS, TILES, PAIRS], F32)
-            by_sin = stage.tile([P, 2 * HEADS, TILES, PAIRS], F32)
+            q_r = rope_banks[g][:].rearrange("p j (h e i) -> p j h e i", h=HEADS, e=2)
             cos_g = cos_sb[:, tables].unsqueeze(2)
-            sin_g = sin_sb[:, tables].unsqueeze(2)
-            minus_sin_g = minus_sin[:, tables].unsqueeze(2)
-            nc.vector.tensor_tensor(
-                out=by_cos[:].rearrange("p a j i -> p j a i"),
-                in0=q_r,
-                in1=cos_g.to_broadcast([P, TILES, 2 * HEADS, PAIRS]),
-                op=MULT,
-            )
-            nc.vector.tensor_tensor(
-                out=by_sin[:, 0:HEADS].rearrange("p h j i -> p j h i"),
-                in0=q_r[:, :, HEADS:, :],
-                in1=minus_sin_g.to_broadcast([P, TILES, HEADS, PAIRS]),
-                op=MULT,
-            )
-            nc.vector.tensor_tensor(
-                out=by_sin[:, HEADS:].rearrange("p h j i -> p j h i"),
-                in0=q_r[:, :, 0:HEADS, :],
-                in1=sin_g.to_broadcast([P, TILES, HEADS, PAIRS]),
-                op=MULT,
-            )
-            products[g] = (by_cos, by_sin)
+            products[g] = []
+            for h in range(HEADS):
+                by_cos = planes.tile([P, 2, TILES, PAIRS], F32)
+                by_sin = planes.tile([P, 2, TILES, PAIRS], F32)
+                nc.vector.tensor_tensor(
+                    out=by_cos[:].rearrange("p e j i -> p j e i"),
+                    in0=q_r[:, :, h],
+                    in1=cos_g.to_broadcast([P, TILES, 2, PAIRS]),
+                    op=MULT,
+                )
+                nc.vector.tensor_tensor(
+                    out=by_sin[:, 0], in0=q_r[:, :, h, 1], in1=minus_sin[:, tables], op=MULT
+                )
+                nc.vector.tensor_tensor(
+                    out=by_sin[:, 1], in0=q_r[:, :, h, 0], in1=sin_sb[:, tables], op=MULT
+                )
+                products[g].append((by_cos, by_sin))
 
         def rotary_sums_and_stores(g):
-            by_cos, by_sin = products[g]
             res = result_tiles[g]
             position = (g % SEQ_GROUPS) * GROUP
             for h in range(HEADS):
+                by_cos, by_sin = products[g][h]
                 nc.gpsimd.tensor_tensor(
                     out=res[:, h, :, DH:].rearrange("p j (i e) -> p j i e", e=2),
-                    in0=by_cos[:].rearrange("p (e h) j i -> p h j i e", e=2)[:, h],
-                    in1=by_sin[:].rearrange("p (e h) j i -> p h j i e", e=2)[:, h],
+                    in0=by_cos[:].rearrange("p e j i -> p j i e"),
+                    in1=by_sin[:].rearrange("p e j i -> p j i e"),
                     op=ADD,
                 )
                 rows = out[g // SEQ_GROUPS, h, position : position + GROUP, :]

from contextlib import ExitStack

import concourse.mybir as mybir
from concourse.masks import make_identity

F32 = mybir.dt.float32
BF16 = mybir.dt.bfloat16
U32 = mybir.dt.uint32
U8 = mybir.dt.uint8
FP8X4 = mybir.dt.float8_e4m3fn_x4
MULT = mybir.AluOpType.mult
ADD = mybir.AluOpType.add

P = 128
PACK = 4
BANK = 512
PSUM_BANKS = 8

BATCH, SEQ, D = 2, 4096, 512
DQ = 512
HEADS, DH, DR = 2, 128, 64
PAIRS = DR // 2
N_UP = HEADS * DH
N_ROPE = HEADS * DR
D_OUT = DH + DR
WORDS = D // 2

TILES = BANK // N_ROPE
GROUP = TILES * P
N_GROUPS = BATCH * SEQ // GROUP
SEQ_GROUPS = SEQ // GROUP
HALVES = 2
HALF_TILES = TILES // HALVES

FLOPS = 2 * BATCH * SEQ * (D * DQ + DQ * (N_UP + N_ROPE))


def tile_multiheadlatentattention_pa_t_kernel(
    tc, x, W_q_down, W_q_up, W_q_rope, rope_cos, rope_sin, out
):
    nc = tc.nc
    x_rows = x.flatten_outer_dims()

    with ExitStack() as ctx:
        consts = ctx.enter_context(tc.tile_pool(name="consts", bufs=1))
        x_pool = ctx.enter_context(tc.tile_pool(name="x_pool", bufs=N_GROUPS))
        stage = ctx.enter_context(tc.tile_pool(name="stage", bufs=3))
        planes = ctx.enter_context(tc.tile_pool(name="planes", bufs=2 * HEADS))
        packed = ctx.enter_context(tc.tile_pool(name="packed", bufs=6))
        results = ctx.enter_context(tc.tile_pool(name="results", bufs=5))
        psum = ctx.enter_context(tc.psum_pool(name="psum", bufs=PSUM_BANKS))
        ctx.enter_context(tc.manual_schedule())

        x_tiles = []

        def load_x(g):
            x_sb = x_pool.tile([P, TILES * D], BF16)
            rows = x_rows[g * GROUP : (g + 1) * GROUP, :]
            nc.sync.dma_start(out=x_sb[:], in_=rows.rearrange("(p j) k -> p (j k)", j=TILES))
            x_tiles.append(x_sb)

        raw_down = consts.tile([P, PACK, DQ], BF16)
        nc.sync.dma_start(
            out=raw_down[:].rearrange("p (u m) f -> p u (m f)", u=2),
            in_=W_q_down.rearrange("(u p m) f -> p u (m f)", u=2, m=2),
        )
        load_x(0)
        raw_up = consts.tile([P, PACK, N_UP], BF16)
        nc.sync.dma_start(out=raw_up[:], in_=W_q_up.rearrange("(p k) n -> p k n", k=PACK))
        raw_rope = consts.tile([P, PACK, N_ROPE], BF16)
        nc.sync.dma_start(out=raw_rope[:], in_=W_q_rope.rearrange("(p k) n -> p k n", k=PACK))
        load_x(1)
        cos_sb = consts.tile([P, SEQ_GROUPS, TILES, PAIRS], BF16)
        nc.sync.dma_start(
            out=cos_sb[:].rearrange("p g j i -> p g (j i)"),
            in_=rope_cos.rearrange("(g p j) i -> p g (j i)", p=P, j=TILES),
        )
        sin_sb = consts.tile([P, SEQ_GROUPS, TILES, PAIRS], BF16)
        nc.sync.dma_start(
            out=sin_sb[:].rearrange("p g j i -> p g (j i)"),
            in_=rope_sin.rearrange("(g p j) i -> p g (j i)", p=P, j=TILES),
        )
        for g in range(2, N_GROUPS):
            load_x(g)

        identity = consts.tile([P, P], F32)
        make_identity(nc, identity[:])

        grouped_down = consts.tile([P, PACK, P, PACK], BF16, align_bytes=64)
        down_view = raw_down[:].rearrange("p k (q t) -> p t q k", t=PACK)
        nc.vector.tensor_copy(out=grouped_down[:, 0:2], in_=down_view[:, 0:2])
        nc.scalar.copy(out=grouped_down[:, 2:4], in_=down_view[:, 2:4])
        down_codes = consts.tile([P, DQ], U32, align_bytes=64)
        down_scales = consts.tile([P, DQ], U8, align_bytes=64)
        nc.vector.quantize_mx(
            out=down_codes[:].bitcast(FP8X4),
            scales=down_scales[:],
            in_=grouped_down[:].rearrange("p t q k -> p (t q k)"),
        )

        grouped_up = consts.tile([P, N_UP, PACK], BF16, align_bytes=64)
        nc.scalar.copy(out=grouped_up[:], in_=raw_up[:].rearrange("p k n -> p n k"))
        grouped_rope = consts.tile([P, N_ROPE, PACK], BF16, align_bytes=64)
        for h in range(HEADS):
            nc.scalar.copy(
                out=grouped_rope[:, h * DR : (h + 1) * DR, :].rearrange("p (e i) k -> p e i k", e=2),
                in_=raw_rope[:, :, h * DR : (h + 1) * DR].rearrange("p k (i e) -> p e i k", e=2),
            )
        second_codes = consts.tile([P, N_UP + N_ROPE], U32, align_bytes=64)
        second_scales = consts.tile([P, N_UP + N_ROPE], U8, align_bytes=64)
        minus_sin = consts.tile([P, SEQ_GROUPS, TILES, PAIRS], BF16)

        def prepare_second_weights():
            nc.vector.quantize_mx(
                out=second_codes[:, 0:N_UP].bitcast(FP8X4),
                scales=second_scales[:, 0:N_UP],
                in_=grouped_up[:].rearrange("p n k -> p (n k)"),
            )
            nc.vector.quantize_mx(
                out=second_codes[:, N_UP:].bitcast(FP8X4),
                scales=second_scales[:, N_UP:],
                in_=grouped_rope[:].rearrange("p n k -> p (n k)"),
            )
            nc.vector.tensor_scalar_mul(out=minus_sin[:], in0=sin_sb[:], scalar1=-1.0)

        x_banks, x_grouped, x_packed = {}, {}, {}
        latent_grouped, latent_packed = {}, {}
        plain_banks, rope_banks, products, result_tiles = {}, {}, {}, {}

        def transpose_x(g):
            words = x_tiles[g][:].bitcast(F32)
            x_banks[g] = []
            for half in range(HALVES):
                xt = psum.tile([P, HALF_TILES, 2, P], F32, tag="bank")
                for jj in range(HALF_TILES):
                    for u in range(2):
                        word = (half * HALF_TILES + jj) * WORDS + u * P
                        nc.tensor.transpose(xt[:, jj, u, :], words[:, word : word + P], identity[:])
                x_banks[g].append(xt)

        def copy_x(g):
            gx = stage.tile([P, GROUP * PACK], BF16, align_bytes=64)
            gx_words = gx[:].bitcast(F32).rearrange("p (j r u) -> p j r u", j=TILES, u=2)
            for half in range(HALVES):
                nc.vector.tensor_copy(
                    out=gx_words[:, half * HALF_TILES : (half + 1) * HALF_TILES],
                    in_=x_banks[g][half][:].rearrange("p j u r -> p j r u"),
                )
            x_grouped[g] = gx

        def quantise(grouped):
            codes = packed.tile([P, GROUP], U32, align_bytes=64)
            scales = packed.tile([P, GROUP], U8, align_bytes=64)
            half_group = GROUP // HALVES
            for half in range(HALVES):
                tokens = slice(half * half_group, (half + 1) * half_group)
                values = slice(half * half_group * PACK, (half + 1) * half_group * PACK)
                nc.vector.quantize_mx(
                    out=codes[:, tokens].bitcast(FP8X4),
                    scales=scales[:, tokens],
                    in_=grouped[:, values],
                )
            return codes, scales

        def first_product(g):
            codes, scales = x_packed[g]
            gq = stage.tile([P, GROUP * PACK], BF16, align_bytes=64)
            for j in range(TILES):
                tokens = slice(j * P, (j + 1) * P)
                latent = psum.tile([P, PACK, P], F32, tag="bank")
                for t in range(PACK):
                    features = slice(t * P, (t + 1) * P)
                    nc.tensor.matmul_mx(
                        out=latent[:, t, :],
                        lhsT=down_codes[:, features].bitcast(FP8X4),
                        lhsT_scale=down_scales[:, features],
                        rhs=codes[:, tokens].bitcast(FP8X4),
                        rhs_scale=scales[:, tokens],
                        start=True,
                        stop=True,
                    )
                nc.scalar.copy(
                    out=gq[:, j * BANK : (j + 1) * BANK].rearrange("p (r t) -> p r t", t=PACK),
                    in_=latent[:].rearrange("p t r -> p r t"),
                )
            latent_grouped[g] = gq

        def second_products(g):
            codes, scales = latent_packed[g]
            plain_banks[g] = []
            rope_bank = psum.tile([P, TILES, N_ROPE], F32, tag="bank")
            for j in range(TILES):
                tokens = slice(j * P, (j + 1) * P)
                if j % HALF_TILES == 0:
                    plain_bank = psum.tile([P, HALF_TILES, N_UP], F32, tag="bank")
                    plain_banks[g].append(plain_bank)
                nc.tensor.matmul_mx(
                    out=plain_bank[:, j % HALF_TILES, :],
                    lhsT=codes[:, tokens].bitcast(FP8X4),
                    lhsT_scale=scales[:, tokens],
                    rhs=second_codes[:, 0:N_UP].bitcast(FP8X4),
                    rhs_scale=second_scales[:, 0:N_UP],
                    start=True,
                    stop=True,
                )
                nc.tensor.matmul_mx(
                    out=rope_bank[:, j, :],
                    lhsT=codes[:, tokens].bitcast(FP8X4),
                    lhsT_scale=scales[:, tokens],
                    rhs=second_codes[:, N_UP:].bitcast(FP8X4),
                    rhs_scale=second_scales[:, N_UP:],
                    start=True,
                    stop=True,
                )
            rope_banks[g] = rope_bank

        def copy_plain(g):
            res = results.tile([P, HEADS, TILES, D_OUT], F32)
            for half in range(HALVES):
                tiles = slice(half * HALF_TILES, (half + 1) * HALF_TILES)
                nc.scalar.copy(
                    out=res[:, :, tiles, 0:DH].rearrange("p h j c -> p j h c"),
                    in_=plain_banks[g][half][:].rearrange("p j (h c) -> p j h c", h=HEADS),
                )
            result_tiles[g] = res

        def rotary_products(g):
            tables = g % SEQ_GROUPS
            q_r = rope_banks[g][:].rearrange("p j (h e i) -> p j h e i", h=HEADS, e=2)
            cos_g = cos_sb[:, tables].unsqueeze(2)
            products[g] = []
            for h in range(HEADS):
                by_cos = planes.tile([P, 2, TILES, PAIRS], F32)
                by_sin = planes.tile([P, 2, TILES, PAIRS], F32)
                nc.vector.tensor_tensor(
                    out=by_cos[:].rearrange("p e j i -> p j e i"),
                    in0=q_r[:, :, h],
                    in1=cos_g.to_broadcast([P, TILES, 2, PAIRS]),
                    op=MULT,
                )
                nc.vector.tensor_tensor(
                    out=by_sin[:, 0], in0=q_r[:, :, h, 1], in1=minus_sin[:, tables], op=MULT
                )
                nc.vector.tensor_tensor(
                    out=by_sin[:, 1], in0=q_r[:, :, h, 0], in1=sin_sb[:, tables], op=MULT
                )
                products[g].append((by_cos, by_sin))

        def rotary_sums_and_stores(g):
            res = result_tiles[g]
            position = (g % SEQ_GROUPS) * GROUP
            for h in range(HEADS):
                by_cos, by_sin = products[g][h]
                nc.gpsimd.tensor_tensor(
                    out=res[:, h, :, DH:].rearrange("p j (i e) -> p j i e", e=2),
                    in0=by_cos[:].rearrange("p e j i -> p j i e"),
                    in1=by_sin[:].rearrange("p e j i -> p j i e"),
                    op=ADD,
                )
                rows = out[g // SEQ_GROUPS, h, position : position + GROUP, :]
                nc.sync.dma_start(
                    out=rows.rearrange("(p j) c -> p (j c)", j=TILES),
                    in_=res[:, h].rearrange("p j c -> p (j c)"),
                )

        def live(g):
            return 0 <= g < N_GROUPS

        def step(n):
            if live(n + 2):
                transpose_x(n + 2)
            if live(n - 2):
                rotary_products(n - 2)
                copy_plain(n - 2)
                rotary_sums_and_stores(n - 2)
            if live(n + 1):
                first_product(n + 1)
            if live(n + 2):
                copy_x(n + 2)
            if live(n - 1):
                second_products(n - 1)
            if live(n + 2):
                x_packed[n + 2] = quantise(x_grouped[n + 2])
            if live(n):
                latent_packed[n] = quantise(latent_grouped[n])

        step(-2)
        step(-1)
        prepare_second_weights()
        for n in range(N_GROUPS + 2):
            step(n)
